import numpy as np
import ml_dtypes


def mxq(x, axis, fmt="e4m3"):
    dtype, down = {"e4m3": (ml_dtypes.float8_e4m3fn, 7), "e5m2": (ml_dtypes.float8_e5m2, 14)}[fmt]
    v = np.moveaxis(np.asarray(x, np.float32).astype(ml_dtypes.bfloat16).astype(np.float64), axis, -1)
    blocks = v.reshape(v.shape[:-1] + (-1, 32))
    amax = np.abs(blocks).max(-1, keepdims=True)
    byte = np.maximum(np.where(amax > 0, np.frexp(amax)[1] - 1 + 127, 0) - down, 1)
    scale = np.exp2(byte - 127.0)
    codes = (blocks / scale).astype(np.float32).astype(dtype).astype(np.float64)
    return np.moveaxis((codes * scale).reshape(v.shape), -1, axis)


WIDE = False


def mx_kscale(k):
    if not WIDE:
        return np.ones(k)
    levels = np.array([10, -10, 5, -5, 0])
    if k % 512:
        return np.exp2(np.random.permutation(np.resize(levels, k // 32))).repeat(32)
    a = np.empty((k // 512, 16))
    for p in range(k // 512):
        a[p, :8] = np.random.permutation(np.resize(levels, 8))
        for g in range(8):
            far = levels[np.abs(levels - a[p, g]) >= 10]
            a[p, g + 8] = far[np.random.randint(len(far))]
    return np.exp2(a.ravel()).repeat(32)


BF16 = ml_dtypes.bfloat16


def bf(x):
    return np.asarray(x, np.float32).astype(BF16)


def f64(x):
    return np.asarray(x).astype(np.float64)


B, S, C, H, D = 8, 1024, 256, 4, 128
E = H * D
EPS = 1e-15


def setup_inputs():
    t = mx_kscale(E)
    return {"q_feat": bf(np.maximum(np.random.standard_normal((B, H, S, D)), 0.0)),
            "vk": bf(np.random.standard_normal((B, H, D, D)) * np.sqrt(S) * t.reshape(H, D)[None, :, :, None]),
            "k_sum": bf(S * (0.11 + 0.02 * np.random.standard_normal((B, H, D)))),
            "Wo": bf(np.random.standard_normal((C, E)) * 6.0 / np.sqrt(E) / t[None, :]),
            "bo": bf(np.random.standard_normal(C) * 0.1)}


def reference(q_feat, vk, k_sum, Wo, bo):
    hs = f64(vk) @ f64(q_feat).transpose(0, 1, 3, 2)
    den = (f64(q_feat) * f64(k_sum)[:, :, None, :]).sum(-1)
    hs = hs / (den[:, :, None, :] + EPS)
    a = hs.transpose(0, 3, 1, 2).reshape(B, S, E)
    return (mxq(a, 2, "e4m3") @ mxq(f64(Wo), 1, "e4m3").T) + f64(bo)

@@ -1,0 +1,222 @@
+from contextlib import ExitStack
+
+import concourse.masks as masks
+import concourse.mybir as mybir
+
+BF16 = mybir.dt.bfloat16
+F32 = mybir.dt.float32
+U32 = mybir.dt.uint32
+U8 = mybir.dt.uint8
+FP8X4 = mybir.dt.float8_e4m3fn_x4
+MULT = mybir.AluOpType.mult
+ADD = mybir.AluOpType.add
+
+B, H, S, D, C = 8, 4, 1024, 128, 256
+E = H * D
+EPS = 1e-15
+
+P = 128
+PACK = 4
+HALVES = 2
+TILES = S // P
+PAIR = 2
+PAIRS = TILES // PAIR
+STEPS = B * PAIRS
+HEADS = B * H
+C_TILES = C // P
+
+assert E == P * PACK
+assert H == PAIRS
+
+FLOPS = 2 * B * S * E * C + 2 * B * H * S * D * D + 2 * B * H * S * D
+
+
+def tile_lineartransformerblock_pc_t_kernel(tc, q_feat, vk, k_sum, Wo, bo, out):
+    nc = tc.nc
+    with ExitStack() as ctx:
+        const = ctx.enter_context(tc.tile_pool(name="const", bufs=1))
+        loads = ctx.enter_context(tc.tile_pool(name="loads", bufs=1))
+        per_batch = ctx.enter_context(tc.tile_pool(name="per_batch", bufs=3))
+        per_pair = ctx.enter_context(tc.tile_pool(name="per_pair", bufs=3))
+        psum = ctx.enter_context(tc.psum_pool(name="psum", bufs=1))
+        ctx.enter_context(tc.manual_schedule())
+
+        ident = const.tile([P, P], BF16)
+        masks.make_identity(nc, ident[:])
+        ident_words = const.tile([P, P], F32)
+        masks.make_identity(nc, ident_words[:])
+
+        ks_rows = const.tile([P, D], BF16)
+        nc.vector.memset(ks_rows[:], 0.0)
+        nc.sync.dma_start(out=ks_rows[0:HEADS, :], in_=k_sum.rearrange("b h d -> (b h) d"))
+
+        wo_sb = const.tile([P, C_TILES, E], BF16)
+        nc.sync.dma_start(out=wo_sb[:], in_=Wo.rearrange("(k p) e -> p k e", p=P))
+
+        vk_sb = {}
+        q_sb = {}
+
+        def load_batch(b):
+            vk_sb[b] = loads.tile([P, H, D], BF16, name="vk_sb%d" % b)
+            nc.sync.dma_start(out=vk_sb[b][:], in_=vk[b].rearrange("h n d -> n h d"))
+            for h in range(H):
+                q_sb[b * H + h] = loads.tile([P, TILES, D], BF16, name="q_sb%d" % (b * H + h))
+                nc.sync.dma_start(
+                    out=q_sb[b * H + h][:], in_=q_feat[b, h].rearrange("(p i) d -> p i d", i=TILES)
+                )
+
+        load_batch(0)
+        load_batch(1)
+        bo_rows = const.tile([P, C], BF16)
+        nc.sync.dma_start(out=bo_rows[:], in_=bo.partition_broadcast(P))
+        bias = const.tile([P, C], F32)
+        nc.gpsimd.tensor_copy(out=bias[:], in_=bo_rows[:])
+        for b in range(2, B):
+            load_batch(b)
+
+        vkT = {}
+        qT = {}
+        den_ps = {}
+        rden = {}
+        a_sb = {}
+        grouped = {}
+        codes = {}
+        scales = {}
+        o_ps = {}
+
+        def flip_vk(b):
+            bank = psum.tile([P, TILES, P], BF16, tag="qT_ps", bufs=2)
+            for h in range(H):
+                nc.tensor.transpose(bank[:, h, :], vk_sb[b][:, h, :], ident[:])
+            vkT[b] = per_batch.tile([P, H, D], BF16, name="vkT", tag="vkT")
+            nc.scalar.copy(out=vkT[b][:].bitcast(F32), in_=bank[:, 0:H, :].bitcast(F32))
+
+        def flip_q(unit):
+            b, h = divmod(unit, H)
+            if h == 0:
+                qT[b] = per_batch.tile([P, H, TILES, P], BF16, name="qT", tag="qT")
+            bank = psum.tile([P, TILES, P], BF16, tag="qT_ps", bufs=2)
+            for i in range(TILES):
+                nc.tensor.transpose(bank[:, i, :], q_sb[unit][:, i, :], ident[:])
+            nc.scalar.copy(out=qT[b][:, h, :, :].bitcast(F32), in_=bank[:].bitcast(F32))
+
+        def denominators(unit):
+            b, h = divmod(unit, H)
+            if h == 0:
+                den_ps[b] = psum.tile([P, TILES, H], F32, name="den_ps", tag="den_ps")
+            for i in range(TILES):
+                nc.tensor.matmul(
+                    den_ps[b][:, i, h : h + 1],
+                    lhsT=qT[b][:, h, i, :],
+                    rhs=ksT[:, unit : unit + 1],
+                    start=True,
+                    stop=True,
+                )
+            if h == H - 1:
+                den_sb = per_batch.tile([P, TILES, H], F32, tag="den_sb")
+                nc.vector.tensor_scalar_add(out=den_sb[:], in0=den_ps[b][:], scalar1=EPS)
+                rden[b] = per_batch.tile([P, TILES, H], F32, name="rden", tag="rden")
+                nc.vector.reciprocal(out=rden[b][:], in_=den_sb[:])
+
+        def read_out(n):
+            b, r = divmod(n, PAIRS)
+            a_sb[n] = per_pair.tile([P, PAIR, E], BF16, name="a_sb", tag="a_sb")
+            for j in range(PAIR):
+                i = r * PAIR + j
+                hs_ps = psum.tile([P, H, D], F32, tag="hs_ps", bufs=2)
+                for h in range(H):
+                    nc.tensor.matmul(
+                        hs_ps[:, h, :], lhsT=qT[b][:, h, i, :], rhs=vkT[b][:, h, :], start=True, stop=True
+                    )
+                nc.vector.tensor_tensor(
+                    out=a_sb[n][:, j, :].rearrange("p (h n) -> p h n", h=H),
+                    in0=hs_ps[:],
+                    in1=rden[b][:, i, :].unsqueeze(2).to_broadcast([P, H, D]),
+                    op=MULT,
+                )
+
+        def flip_a(n):
+            bank = psum.tile([P, PAIR, HALVES, P], F32, tag="aT_ps")
+            for j in range(PAIR):
+                words = a_sb[n][:, j, :].bitcast(F32)
+                for u in range(HALVES):
+                    nc.tensor.transpose(bank[:, j, u, :], words[:, u : HALVES * P : HALVES], ident_words[:])
+            grouped[n] = per_pair.tile([P, PAIR, P, PACK], BF16, name="grouped", tag="grouped", align_bytes=64)
+            nc.scalar.copy(out=grouped[n][:].bitcast(F32), in_=bank[:].rearrange("p j u s -> p j s u"))
+
+        def quantise(n):
+            codes[n] = per_pair.tile([P, PAIR * P], U32, name="codes", tag="codes", align_bytes=64)
+            scales[n] = per_pair.tile([P, PAIR * P], U8, name="scales", tag="scales", align_bytes=64)
+            nc.vector.quantize_mx(
+                out=codes[n][:].bitcast(FP8X4),
+                scales=scales[n][:],
+                in_=grouped[n][:].rearrange("p j s t -> p (j s t)"),
+            )
+
+        def project(n):
+            o_ps[n] = psum.tile([P, PAIR, C], F32, name="o_ps", tag="o_ps", bufs=2)
+            for j in range(PAIR):
+                tokens = slice(j * P, (j + 1) * P)
+                nc.tensor.matmul_mx(
+                    out=o_ps[n][:, j, :],
+                    lhsT=codes[n][:, tokens].bitcast(FP8X4),
+                    lhsT_scale=scales[n][:, tokens],
+                    rhs=wo_codes[:].bitcast(FP8X4),
+                    rhs_scale=wo_scales[:],
+                    start=True,
+                    stop=True,
+                )
+
+        def finish(n):
+            b, r = divmod(n, PAIRS)
+            o_sb = per_pair.tile([P, PAIR, C], F32, tag="o_sb", bufs=4)
+            nc.scalar.copy(out=o_sb[:], in_=o_ps[n][:])
+            nc.gpsimd.tensor_tensor(
+                out=o_sb[:], in0=o_sb[:], in1=bias[:].unsqueeze(1).to_broadcast([P, PAIR, C]), op=ADD
+            )
+            rows = out[b].rearrange("(p i) c -> p i c", i=TILES)
+            nc.sync.dma_start(out=rows[:, r * PAIR : (r + 1) * PAIR, :], in_=o_sb[:])
+
+        bank = psum.tile([P, TILES, P], BF16, tag="qT_ps", bufs=2)
+        nc.tensor.transpose(bank[:, 0, :], ks_rows[:], ident[:])
+        ksT = const.tile([P, HEADS], BF16)
+        nc.scalar.copy(out=ksT[:], in_=bank[:, 0, 0:HEADS])
+
+        wo_bank = psum.tile([P, HALVES, C], F32, tag="aT_ps")
+        for k in range(C_TILES):
+            words = wo_sb[:, k, :].bitcast(F32)
+            for u in range(HALVES):
+                nc.tensor.transpose(
+                    wo_bank[:, u, k * P : (k + 1) * P], words[:, u : HALVES * P : HALVES], ident_words[:]
+                )
+        wo_grouped = const.tile([P, C, PACK], BF16, align_bytes=64)
+        nc.scalar.copy(out=wo_grouped[:].bitcast(F32), in_=wo_bank[:].rearrange("p u c -> p c u"))
+        wo_codes = const.tile([P, C], U32, align_bytes=64)
+        wo_scales = const.tile([P, C], U8, align_bytes=64)
+        nc.vector.quantize_mx(
+            out=wo_codes[:].bitcast(FP8X4), scales=wo_scales[:], in_=wo_grouped[:].rearrange("p c t -> p (c t)")
+        )
+
+        flip_vk(0)
+        for unit in range(H + 1):
+            flip_q(unit)
+        for unit in range(H):
+            denominators(unit)
+
+        for n in range(STEPS + 2):
+            b, r = divmod(n, PAIRS)
+            if n >= 2:
+                quantise(n - 2)
+            if n < STEPS:
+                read_out(n)
+            if n + H + 1 < HEADS:
+                flip_q(n + H + 1)
+            if r == 0 and b + 1 < B:
+                flip_vk(b + 1)
+            if 1 <= n < STEPS + 1:
+                flip_a(n - 1)
+            if n >= 2:
+                project(n - 2)
+                finish(n - 2)
+            if n + H < HEADS:
+                denominators(n + H)

@@ -89,7 +89,10 @@ def tile_lineartransformerblock_pc_t_kernel(tc, q_feat, vk, k_sum, Wo, bo, out):
             for h in range(H):
                 nc.tensor.transpose(bank[:, h, :], vk_sb[b][:, h, :], ident[:])
             vkT[b] = per_batch.tile([P, H, D], BF16, name="vkT", tag="vkT")
-            nc.scalar.copy(out=vkT[b][:].bitcast(F32), in_=bank[:, 0:H, :].bitcast(F32))
+            nc.scalar.copy(
+                out=vkT[b][:].bitcast(F32).rearrange("p h (u m) -> p h u m", u=HALVES),
+                in_=bank[:, 0:H, :].bitcast(F32).rearrange("p h (m u) -> p h u m", u=HALVES),
+            )
 
         def flip_q(unit):
             b, h = divmod(unit, H)
@@ -129,9 +132,9 @@ def tile_lineartransformerblock_pc_t_kernel(tc, q_feat, vk, k_sum, Wo, bo, out):
                         hs_ps[:, h, :], lhsT=qT[b][:, h, i, :], rhs=vkT[b][:, h, :], start=True, stop=True
                     )
                 nc.vector.tensor_tensor(
-                    out=a_sb[n][:, j, :].rearrange("p (h n) -> p h n", h=H),
-                    in0=hs_ps[:],
-                    in1=rden[b][:, i, :].unsqueeze(2).to_broadcast([P, H, D]),
+                    out=a_sb[n][:, j, :].rearrange("p (u h k) -> p h u k", u=HALVES, h=H),
+                    in0=hs_ps[:].rearrange("p h (u k) -> p h u k", u=HALVES),
+                    in1=rden[b][:, i, :].unsqueeze(2).unsqueeze(3).to_broadcast([P, H, HALVES, D // HALVES]),
                     op=MULT,
                 )
 
@@ -140,7 +143,7 @@ def tile_lineartransformerblock_pc_t_kernel(tc, q_feat, vk, k_sum, Wo, bo, out):
             for j in range(PAIR):
                 words = a_sb[n][:, j, :].bitcast(F32)
                 for u in range(HALVES):
-                    nc.tensor.transpose(bank[:, j, u, :], words[:, u : HALVES * P : HALVES], ident_words[:])
+                    nc.tensor.transpose(bank[:, j, u, :], words[:, u * P : (u + 1) * P], ident_words[:])
             grouped[n] = per_pair.tile([P, PAIR, P, PACK], BF16, name="grouped", tag="grouped", align_bytes=64)
             nc.scalar.copy(out=grouped[n][:].bitcast(F32), in_=bank[:].rearrange("p j u s -> p j s u"))
 

@@ -10,6 +10,7 @@ U8 = mybir.dt.uint8
 FP8X4 = mybir.dt.float8_e4m3fn_x4
 MULT = mybir.AluOpType.mult
 ADD = mybir.AluOpType.add
+COPY = mybir.ActivationFunctionType.Copy
 
 B, H, S, D, C = 8, 4, 1024, 128, 256
 E = H * D
@@ -131,6 +132,15 @@ def tile_lineartransformerblock_pc_t_kernel(tc, q_feat, vk, k_sum, Wo, bo, out):
                     nc.tensor.matmul(
                         hs_ps[:, h, :], lhsT=qT[b][:, h, i, :], rhs=vkT[b][:, h, :], start=True, stop=True
                     )
+                if j == 1 and n % 2 == 1:
+                    for h in range(H):
+                        nc.scalar.activation(
+                            out=a_sb[n][:, j, :].rearrange("p (u h k) -> p h u k", u=HALVES, h=H)[:, h, :, :],
+                            in_=hs_ps[:, h, :].rearrange("p (u k) -> p u k", u=HALVES),
+                            func=COPY,
+                            scale=rden[b][:, i, h : h + 1],
+                        )
+                    continue
                 nc.vector.tensor_tensor(
                     out=a_sb[n][:, j, :].rearrange("p (u h k) -> p h u k", u=HALVES, h=H),
                     in0=hs_ps[:].rearrange("p h (u k) -> p h u k", u=HALVES),
@@ -173,9 +183,8 @@ def tile_lineartransformerblock_pc_t_kernel(tc, q_feat, vk, k_sum, Wo, bo, out):
         def finish(n):
             b, r = divmod(n, PAIRS)
             o_sb = per_pair.tile([P, PAIR, C], F32, tag="o_sb", bufs=4)
-            nc.scalar.copy(out=o_sb[:], in_=o_ps[n][:])
-            nc.gpsimd.tensor_tensor(
-                out=o_sb[:], in0=o_sb[:], in1=bias[:].unsqueeze(1).to_broadcast([P, PAIR, C]), op=ADD
+            nc.vector.tensor_tensor(
+                out=o_sb[:], in0=o_ps[n][:], in1=bias[:].unsqueeze(1).to_broadcast([P, PAIR, C]), op=ADD
             )
             rows = out[b].rearrange("(p i) c -> p i c", i=TILES)
             nc.sync.dma_start(out=rows[:, r * PAIR : (r + 1) * PAIR, :], in_=o_sb[:])

@@ -10,7 +10,6 @@ U8 = mybir.dt.uint8
 FP8X4 = mybir.dt.float8_e4m3fn_x4
 MULT = mybir.AluOpType.mult
 ADD = mybir.AluOpType.add
-COPY = mybir.ActivationFunctionType.Copy
 
 B, H, S, D, C = 8, 4, 1024, 128, 256
 E = H * D
@@ -127,20 +126,11 @@ def tile_lineartransformerblock_pc_t_kernel(tc, q_feat, vk, k_sum, Wo, bo, out):
             a_sb[n] = per_pair.tile([P, PAIR, E], BF16, name="a_sb", tag="a_sb")
             for j in range(PAIR):
                 i = r * PAIR + j
-                hs_ps = psum.tile([P, H, D], F32, tag="hs_ps", bufs=2)
+                hs_ps = psum.tile([P, H, D], F32, tag="hs_ps", bufs=3)
                 for h in range(H):
                     nc.tensor.matmul(
                         hs_ps[:, h, :], lhsT=qT[b][:, h, i, :], rhs=vkT[b][:, h, :], start=True, stop=True
                     )
-                if j == 1 and n % 2 == 1:
-                    for h in range(H):
-                        nc.scalar.activation(
-                            out=a_sb[n][:, j, :].rearrange("p (u h k) -> p h u k", u=HALVES, h=H)[:, h, :, :],
-                            in_=hs_ps[:, h, :].rearrange("p (u k) -> p u k", u=HALVES),
-                            func=COPY,
-                            scale=rden[b][:, i, h : h + 1],
-                        )
-                    continue
                 nc.vector.tensor_tensor(
                     out=a_sb[n][:, j, :].rearrange("p (u h k) -> p h u k", u=HALVES, h=H),
                     in0=hs_ps[:].rearrange("p h (u k) -> p h u k", u=HALVES),
@@ -167,7 +157,7 @@ def tile_lineartransformerblock_pc_t_kernel(tc, q_feat, vk, k_sum, Wo, bo, out):
             )
 
         def project(n):
-            o_ps[n] = psum.tile([P, PAIR, C], F32, name="o_ps", tag="o_ps", bufs=2)
+            o_ps[n] = psum.tile([P, PAIR, C], F32, name="o_ps", tag="o_ps")
             for j in range(PAIR):
                 tokens = slice(j * P, (j + 1) * P)
                 nc.tensor.matmul_mx(
@@ -182,10 +172,13 @@ def tile_lineartransformerblock_pc_t_kernel(tc, q_feat, vk, k_sum, Wo, bo, out):
 
         def finish(n):
             b, r = divmod(n, PAIRS)
-            o_sb = per_pair.tile([P, PAIR, C], F32, tag="o_sb", bufs=4)
-            nc.vector.tensor_tensor(
-                out=o_sb[:], in0=o_ps[n][:], in1=bias[:].unsqueeze(1).to_broadcast([P, PAIR, C]), op=ADD
-            )
+            o_sb = per_pair.tile([P, PAIR, C], F32, tag="o_sb", bufs=12)
+            bias_rows = bias[:].unsqueeze(1).to_broadcast([P, PAIR, C])
+            if n % 4 == 3:
+                nc.vector.tensor_tensor(out=o_sb[:], in0=o_ps[n][:], in1=bias_rows, op=ADD)
+            else:
+                nc.scalar.copy(out=o_sb[:], in_=o_ps[n][:])
+                nc.gpsimd.tensor_tensor(out=o_sb[:], in0=o_sb[:], in1=bias_rows, op=ADD)
             rows = out[b].rearrange("(p i) c -> p i c", i=TILES)
             nc.sync.dma_start(out=rows[:, r * PAIR : (r + 1) * PAIR, :], in_=o_sb[:])
 
@@ -215,9 +208,11 @@ def tile_lineartransformerblock_pc_t_kernel(tc, q_feat, vk, k_sum, Wo, bo, out):
         for unit in range(H):
             denominators(unit)
 
-        for n in range(STEPS + 2):
+        for n in range(STEPS + 3):
             b, r = divmod(n, PAIRS)
-            if n >= 2:
+            if n >= 3:
+                finish(n - 3)
+            if 2 <= n < STEPS + 2:
                 quantise(n - 2)
             if n < STEPS:
                 read_out(n)
@@ -227,8 +222,7 @@ def tile_lineartransformerblock_pc_t_kernel(tc, q_feat, vk, k_sum, Wo, bo, out):
                 flip_vk(b + 1)
             if 1 <= n < STEPS + 1:
                 flip_a(n - 1)
-            if n >= 2:
-                project(n - 2)
-                finish(n - 2)
             if n + H < HEADS:
                 denominators(n + H)
+            if 2 <= n < STEPS + 2:
+                project(n - 2)

@@ -46,33 +46,47 @@ def tile_lineartransformerblock_pc_t_kernel(tc, q_feat, vk, k_sum, Wo, bo, out):
         ident_words = const.tile([P, P], F32)
         masks.make_identity(nc, ident_words[:])
 
+        idle_rows = const.tile([P, PAIR * C], BF16)
+        nc.vector.memset(idle_rows[:], 0.0)
+
+        def keep_clock(times):
+            for k in range(times):
+                bank = psum.tile([P, PAIR * C], F32, tag="hs_ps", bufs=3)
+                nc.tensor.matmul(bank[:], lhsT=idle_rows[:, 0:P], rhs=idle_rows[:], start=True, stop=True)
+
         ks_rows = const.tile([P, D], BF16)
         nc.vector.memset(ks_rows[:], 0.0)
-        nc.sync.dma_start(out=ks_rows[0:HEADS, :], in_=k_sum.rearrange("b h d -> (b h) d"))
 
-        wo_sb = const.tile([P, C_TILES, E], BF16)
-        nc.sync.dma_start(out=wo_sb[:], in_=Wo.rearrange("(k p) e -> p k e", p=P))
+        bo_row = const.tile([P, C], BF16)
+        nc.vector.memset(bo_row[:], 0.0)
+        ones = const.tile([P, P], BF16)
+        nc.vector.memset(ones[:], 1.0)
 
         vk_sb = {}
         q_sb = {}
 
-        def load_batch(b):
+        def load_vk(b):
             vk_sb[b] = loads.tile([P, H, D], BF16, name="vk_sb%d" % b)
             nc.sync.dma_start(out=vk_sb[b][:], in_=vk[b].rearrange("h n d -> n h d"))
-            for h in range(H):
-                q_sb[b * H + h] = loads.tile([P, TILES, D], BF16, name="q_sb%d" % (b * H + h))
-                nc.sync.dma_start(
-                    out=q_sb[b * H + h][:], in_=q_feat[b, h].rearrange("(p i) d -> p i d", i=TILES)
-                )
 
-        load_batch(0)
-        load_batch(1)
-        bo_rows = const.tile([P, C], BF16)
-        nc.sync.dma_start(out=bo_rows[:], in_=bo.partition_broadcast(P))
-        bias = const.tile([P, C], F32)
-        nc.gpsimd.tensor_copy(out=bias[:], in_=bo_rows[:])
-        for b in range(2, B):
-            load_batch(b)
+        def load_q(unit):
+            b, h = divmod(unit, H)
+            q_sb[unit] = loads.tile([P, TILES, D], BF16, name="q_sb%d" % unit)
+            nc.sync.dma_start(out=q_sb[unit][:], in_=q_feat[b, h].rearrange("(p i) d -> p i d", i=TILES))
+
+        load_q(0)
+        load_vk(0)
+        nc.sync.dma_start(out=ks_rows[0:HEADS, :], in_=k_sum.rearrange("b h d -> (b h) d"))
+        load_q(1)
+        wo_sb = const.tile([P, C_TILES, E], BF16)
+        nc.sync.dma_start(out=wo_sb[:], in_=Wo.rearrange("(k p) e -> p k e", p=P))
+        nc.sync.dma_start(out=bo_row[0:1, :], in_=bo.unsqueeze(0))
+        load_q(2)
+        load_q(3)
+        for b in range(1, B):
+            load_vk(b)
+            for h in range(H):
+                load_q(b * H + h)
 
         vkT = {}
         qT = {}
@@ -182,10 +196,16 @@ def tile_lineartransformerblock_pc_t_kernel(tc, q_feat, vk, k_sum, Wo, bo, out):
             rows = out[b].rearrange("(p i) c -> p i c", i=TILES)
             nc.sync.dma_start(out=rows[:, r * PAIR : (r + 1) * PAIR, :], in_=o_sb[:])
 
+        keep_clock(5)
+        flip_q(0)
+        flip_vk(0)
         bank = psum.tile([P, TILES, P], BF16, tag="qT_ps", bufs=2)
         nc.tensor.transpose(bank[:, 0, :], ks_rows[:], ident[:])
         ksT = const.tile([P, HEADS], BF16)
         nc.scalar.copy(out=ksT[:], in_=bank[:, 0, 0:HEADS])
+        keep_clock(1)
+        flip_q(1)
+        keep_clock(1)
 
         wo_bank = psum.tile([P, HALVES, C], F32, tag="aT_ps")
         for k in range(C_TILES):
@@ -195,18 +215,24 @@ def tile_lineartransformerblock_pc_t_kernel(tc, q_feat, vk, k_sum, Wo, bo, out):
                     wo_bank[:, u, k * P : (k + 1) * P], words[:, u : HALVES * P : HALVES], ident_words[:]
                 )
         wo_grouped = const.tile([P, C, PACK], BF16, align_bytes=64)
-        nc.scalar.copy(out=wo_grouped[:].bitcast(F32), in_=wo_bank[:].rearrange("p u c -> p c u"))
+        nc.vector.tensor_copy(out=wo_grouped[:].bitcast(F32), in_=wo_bank[:].rearrange("p u c -> p c u"))
         wo_codes = const.tile([P, C], U32, align_bytes=64)
         wo_scales = const.tile([P, C], U8, align_bytes=64)
+        bias_bank = psum.tile([P, PAIR, C], F32, tag="o_ps")
+        nc.tensor.matmul(bias_bank[:, 0, :], lhsT=ones[:], rhs=bo_row[:], start=True, stop=True)
+        bias = const.tile([P, C], F32)
+        nc.vector.tensor_copy(out=bias[:], in_=bias_bank[:, 0, :])
         nc.vector.quantize_mx(
             out=wo_codes[:].bitcast(FP8X4), scales=wo_scales[:], in_=wo_grouped[:].rearrange("p c t -> p (c t)")
         )
 
-        flip_vk(0)
-        for unit in range(H + 1):
-            flip_q(unit)
-        for unit in range(H):
-            denominators(unit)
+        denominators(0)
+        flip_q(2)
+        denominators(1)
+        keep_clock(1)
+        flip_q(3)
+        denominators(2)
+        denominators(3)
 
         for n in range(STEPS + 3):
             b, r = divmod(n, PAIRS)
@@ -216,6 +242,8 @@ def tile_lineartransformerblock_pc_t_kernel(tc, q_feat, vk, k_sum, Wo, bo, out):
                 quantise(n - 2)
             if n < STEPS:
                 read_out(n)
+            if n == 0:
+                flip_q(H)
             if n + H + 1 < HEADS:
                 flip_q(n + H + 1)
             if r == 0 and b + 1 < B:

@@ -21,7 +21,8 @@ HALVES = 2
 TILES = S // P
 PAIR = 2
 PAIRS = TILES // PAIR
-STEPS = B * PAIRS
+GROUPS = [(k * PAIR, PAIR) for k in range(B * PAIRS - 1)] + [(B * TILES - 2, 1), (B * TILES - 1, 1)]
+LAST = len(GROUPS) - 1
 HEADS = B * H
 C_TILES = C // P
 
@@ -74,8 +75,8 @@ def tile_lineartransformerblock_pc_t_kernel(tc, q_feat, vk, k_sum, Wo, bo, out):
             q_sb[unit] = loads.tile([P, TILES, D], BF16, name="q_sb%d" % unit)
             nc.sync.dma_start(out=q_sb[unit][:], in_=q_feat[b, h].rearrange("(p i) d -> p i d", i=TILES))
 
-        load_q(0)
         load_vk(0)
+        load_q(0)
         nc.sync.dma_start(out=ks_rows[0:HEADS, :], in_=k_sum.rearrange("b h d -> (b h) d"))
         load_q(1)
         wo_sb = const.tile([P, C_TILES, E], BF16)
@@ -136,10 +137,11 @@ def tile_lineartransformerblock_pc_t_kernel(tc, q_feat, vk, k_sum, Wo, bo, out):
                 nc.vector.reciprocal(out=rden[b][:], in_=den_sb[:])
 
         def read_out(n):
-            b, r = divmod(n, PAIRS)
+            first, width = GROUPS[n]
+            b, first = divmod(first, TILES)
             a_sb[n] = per_pair.tile([P, PAIR, E], BF16, name="a_sb", tag="a_sb")
-            for j in range(PAIR):
-                i = r * PAIR + j
+            for j in range(width):
+                i = first + j
                 hs_ps = psum.tile([P, H, D], F32, tag="hs_ps", bufs=3)
                 for h in range(H):
                     nc.tensor.matmul(
@@ -153,26 +155,36 @@ def tile_lineartransformerblock_pc_t_kernel(tc, q_feat, vk, k_sum, Wo, bo, out):
                 )
 
         def flip_a(n):
-            bank = psum.tile([P, PAIR, HALVES, P], F32, tag="aT_ps")
-            for j in range(PAIR):
+            width = GROUPS[n][1]
+            if GROUPS[n][1] < PAIR:
+                bank = psum.tile([P, PAIR, HALVES, P], F32, tag="qT_ps", bufs=2)
+            else:
+                bank = psum.tile([P, PAIR, HALVES, P], F32, tag="aT_ps")
+            for j in range(width):
                 words = a_sb[n][:, j, :].bitcast(F32)
                 for u in range(HALVES):
                     nc.tensor.transpose(bank[:, j, u, :], words[:, u * P : (u + 1) * P], ident_words[:])
             grouped[n] = per_pair.tile([P, PAIR, P, PACK], BF16, name="grouped", tag="grouped", align_bytes=64)
-            nc.scalar.copy(out=grouped[n][:].bitcast(F32), in_=bank[:].rearrange("p j u s -> p j s u"))
+            nc.scalar.copy(
+                out=grouped[n][:, 0:width, :, :].bitcast(F32), in_=bank[:, 0:width, :, :].rearrange("p j u s -> p j s u")
+            )
 
         def quantise(n):
+            tokens = slice(0, GROUPS[n][1] * P)
             codes[n] = per_pair.tile([P, PAIR * P], U32, name="codes", tag="codes", align_bytes=64)
             scales[n] = per_pair.tile([P, PAIR * P], U8, name="scales", tag="scales", align_bytes=64)
             nc.vector.quantize_mx(
-                out=codes[n][:].bitcast(FP8X4),
-                scales=scales[n][:],
-                in_=grouped[n][:].rearrange("p j s t -> p (j s t)"),
+                out=codes[n][:, tokens].bitcast(FP8X4),
+                scales=scales[n][:, tokens],
+                in_=grouped[n][:, 0 : GROUPS[n][1], :, :].rearrange("p j s t -> p (j s t)"),
             )
 
         def project(n):
-            o_ps[n] = psum.tile([P, PAIR, C], F32, name="o_ps", tag="o_ps")
-            for j in range(PAIR):
+            if GROUPS[n][1] < PAIR:
+                o_ps[n] = psum.tile([P, PAIR, C], F32, name="o_ps", tag="hs_ps", bufs=3)
+            else:
+                o_ps[n] = psum.tile([P, PAIR, C], F32, name="o_ps", tag="o_ps")
+            for j in range(GROUPS[n][1]):
                 tokens = slice(j * P, (j + 1) * P)
                 nc.tensor.matmul_mx(
                     out=o_ps[n][:, j, :],
@@ -185,20 +197,23 @@ def tile_lineartransformerblock_pc_t_kernel(tc, q_feat, vk, k_sum, Wo, bo, out):
                 )
 
         def finish(n):
-            b, r = divmod(n, PAIRS)
+            first, width = GROUPS[n]
+            b, first = divmod(first, TILES)
             o_sb = per_pair.tile([P, PAIR, C], F32, tag="o_sb", bufs=12)
-            bias_rows = bias[:].unsqueeze(1).to_broadcast([P, PAIR, C])
-            if n % 4 == 3:
-                nc.vector.tensor_tensor(out=o_sb[:], in0=o_ps[n][:], in1=bias_rows, op=ADD)
+            bias_rows = bias[:].unsqueeze(1).to_broadcast([P, width, C])
+            product = o_ps[n][:, 0:width, :]
+            result = o_sb[:, 0:width, :]
+            if n % 8 == 7 or n >= LAST - 2:
+                nc.vector.tensor_tensor(out=result, in0=product, in1=bias_rows, op=ADD)
             else:
-                nc.scalar.copy(out=o_sb[:], in_=o_ps[n][:])
-                nc.gpsimd.tensor_tensor(out=o_sb[:], in0=o_sb[:], in1=bias_rows, op=ADD)
+                nc.scalar.copy(out=result, in_=product)
+                nc.gpsimd.tensor_tensor(out=result, in0=result, in1=bias_rows, op=ADD)
             rows = out[b].rearrange("(p i) c -> p i c", i=TILES)
-            nc.sync.dma_start(out=rows[:, r * PAIR : (r + 1) * PAIR, :], in_=o_sb[:])
+            nc.sync.dma_start(out=rows[:, first : first + width, :], in_=result)
 
         keep_clock(5)
-        flip_q(0)
         flip_vk(0)
+        flip_q(0)
         bank = psum.tile([P, TILES, P], BF16, tag="qT_ps", bufs=2)
         nc.tensor.transpose(bank[:, 0, :], ks_rows[:], ident[:])
         ksT = const.tile([P, HEADS], BF16)
@@ -234,23 +249,35 @@ def tile_lineartransformerblock_pc_t_kernel(tc, q_feat, vk, k_sum, Wo, bo, out):
         denominators(2)
         denominators(3)
 
-        for n in range(STEPS + 3):
+        for n in range(LAST):
             b, r = divmod(n, PAIRS)
+            if n >= 2:
+                quantise(n - 2)
             if n >= 3:
                 finish(n - 3)
-            if 2 <= n < STEPS + 2:
-                quantise(n - 2)
-            if n < STEPS:
-                read_out(n)
+            read_out(n)
+            if n == LAST - 1:
+                read_out(LAST)
+            if n >= 1:
+                flip_a(n - 1)
             if n == 0:
                 flip_q(H)
             if n + H + 1 < HEADS:
                 flip_q(n + H + 1)
             if r == 0 and b + 1 < B:
                 flip_vk(b + 1)
-            if 1 <= n < STEPS + 1:
-                flip_a(n - 1)
             if n + H < HEADS:
                 denominators(n + H)
-            if 2 <= n < STEPS + 2:
+            if n >= 2:
                 project(n - 2)
+
+        finish(LAST - 3)
+        quantise(LAST - 2)
+        for n in (LAST - 1, LAST):
+            flip_a(n)
+        project(LAST - 2)
+        for n in (LAST - 1, LAST):
+            quantise(n)
+            project(n)
+        for n in (LAST - 2, LAST - 1, LAST):
+            finish(n)

@@ -27,6 +27,7 @@ HEADS = B * H
 C_TILES = C // P
 
 assert E == P * PACK
+assert TILES == PAIR * H
 assert H == PAIRS
 
 FLOPS = 2 * B * S * E * C + 2 * B * H * S * D * D + 2 * B * H * S * D
@@ -90,6 +91,7 @@ def tile_lineartransformerblock_pc_t_kernel(tc, q_feat, vk, k_sum, Wo, bo, out):
                 load_q(b * H + h)
 
         vkT = {}
+        qT_ps = {}
         qT = {}
         den_ps = {}
         rden = {}
@@ -109,14 +111,21 @@ def tile_lineartransformerblock_pc_t_kernel(tc, q_feat, vk, k_sum, Wo, bo, out):
                 in_=bank[:, 0:H, :].bitcast(F32).rearrange("p h (m u) -> p h u m", u=HALVES),
             )
 
-        def flip_q(unit):
+        def flip_q_tile(unit, i):
+            if i == 0:
+                qT_ps[unit] = psum.tile([P, TILES, P], BF16, name="qT_ps", tag="qT_ps", bufs=2)
+            nc.tensor.transpose(qT_ps[unit][:, i, :], q_sb[unit][:, i, :], ident[:])
+
+        def keep_q(unit):
             b, h = divmod(unit, H)
             if h == 0:
                 qT[b] = per_batch.tile([P, H, TILES, P], BF16, name="qT", tag="qT")
-            bank = psum.tile([P, TILES, P], BF16, tag="qT_ps", bufs=2)
+            nc.scalar.copy(out=qT[b][:, h, :, :].bitcast(F32), in_=qT_ps[unit][:].bitcast(F32))
+
+        def flip_q(unit):
             for i in range(TILES):
-                nc.tensor.transpose(bank[:, i, :], q_sb[unit][:, i, :], ident[:])
-            nc.scalar.copy(out=qT[b][:, h, :, :].bitcast(F32), in_=bank[:].bitcast(F32))
+                flip_q_tile(unit, i)
+            keep_q(unit)
 
         def denominators(unit):
             b, h = divmod(unit, H)
@@ -136,7 +145,7 @@ def tile_lineartransformerblock_pc_t_kernel(tc, q_feat, vk, k_sum, Wo, bo, out):
                 rden[b] = per_batch.tile([P, TILES, H], F32, name="rden", tag="rden")
                 nc.vector.reciprocal(out=rden[b][:], in_=den_sb[:])
 
-        def read_out(n):
+        def read_out(n, unit):
             first, width = GROUPS[n]
             b, first = divmod(first, TILES)
             a_sb[n] = per_pair.tile([P, PAIR, E], BF16, name="a_sb", tag="a_sb")
@@ -147,6 +156,8 @@ def tile_lineartransformerblock_pc_t_kernel(tc, q_feat, vk, k_sum, Wo, bo, out):
                     nc.tensor.matmul(
                         hs_ps[:, h, :], lhsT=qT[b][:, h, i, :], rhs=vkT[b][:, h, :], start=True, stop=True
                     )
+                    if unit < HEADS:
+                        flip_q_tile(unit, j * H + h)
                 nc.vector.tensor_tensor(
                     out=a_sb[n][:, j, :].rearrange("p (u h k) -> p h u k", u=HALVES, h=H),
                     in0=hs_ps[:].rearrange("p h (u k) -> p h u k", u=HALVES),
@@ -255,15 +266,15 @@ def tile_lineartransformerblock_pc_t_kernel(tc, q_feat, vk, k_sum, Wo, bo, out):
                 quantise(n - 2)
             if n >= 3:
                 finish(n - 3)
-            read_out(n)
+            read_out(n, n + H + 1)
             if n == LAST - 1:
-                read_out(LAST)
+                read_out(LAST, HEADS)
             if n >= 1:
                 flip_a(n - 1)
             if n == 0:
                 flip_q(H)
             if n + H + 1 < HEADS:
-                flip_q(n + H + 1)
+                keep_q(n + H + 1)
             if r == 0 and b + 1 < B:
                 flip_vk(b + 1)
             if n + H < HEADS:

@@ -80,11 +80,11 @@ def tile_lineartransformerblock_pc_t_kernel(tc, q_feat, vk, k_sum, Wo, bo, out):
         load_q(0)
         nc.sync.dma_start(out=ks_rows[0:HEADS, :], in_=k_sum.rearrange("b h d -> (b h) d"))
         load_q(1)
+        load_q(2)
+        load_q(3)
         wo_sb = const.tile([P, C_TILES, E], BF16)
         nc.sync.dma_start(out=wo_sb[:], in_=Wo.rearrange("(k p) e -> p k e", p=P))
         nc.sync.dma_start(out=bo_row[0:1, :], in_=bo.unsqueeze(0))
-        load_q(2)
-        load_q(3)
         for b in range(1, B):
             load_vk(b)
             for h in range(H):
@@ -94,6 +94,7 @@ def tile_lineartransformerblock_pc_t_kernel(tc, q_feat, vk, k_sum, Wo, bo, out):
         qT_ps = {}
         qT = {}
         den_ps = {}
+        den_sb = {}
         rden = {}
         a_sb = {}
         grouped = {}
@@ -111,41 +112,51 @@ def tile_lineartransformerblock_pc_t_kernel(tc, q_feat, vk, k_sum, Wo, bo, out):
                 in_=bank[:, 0:H, :].bitcast(F32).rearrange("p h (m u) -> p h u m", u=HALVES),
             )
 
-        def flip_q_tile(unit, i):
-            if i == 0:
-                qT_ps[unit] = psum.tile([P, TILES, P], BF16, name="qT_ps", tag="qT_ps", bufs=2)
-            nc.tensor.transpose(qT_ps[unit][:, i, :], q_sb[unit][:, i, :], ident[:])
+        def job_tiles(k):
+            if k < H:
+                return [(0, h, k * PAIR + j) for h in range(H) for j in range(PAIR)]
+            return [(k // H, k % H, i) for i in range(TILES)]
 
-        def keep_q(unit):
-            b, h = divmod(unit, H)
-            if h == 0:
-                qT[b] = per_batch.tile([P, H, TILES, P], BF16, name="qT", tag="qT")
-            nc.scalar.copy(out=qT[b][:, h, :, :].bitcast(F32), in_=qT_ps[unit][:].bitcast(F32))
+        def qT_of(b, h, i):
+            k = i // PAIR if b == 0 else b * H + h
+            return qT[k][:, job_tiles(k).index((b, h, i)), :]
 
-        def flip_q(unit):
-            for i in range(TILES):
-                flip_q_tile(unit, i)
-            keep_q(unit)
+        def flip_q_tile(k, step):
+            if step == 0:
+                qT_ps[k] = psum.tile([P, TILES, P], BF16, name="qT_ps", tag="qT_ps", bufs=2)
+            b, h, i = job_tiles(k)[step]
+            nc.tensor.transpose(qT_ps[k][:, step, :], q_sb[b * H + h][:, i, :], ident[:])
 
-        def denominators(unit):
-            b, h = divmod(unit, H)
-            if h == 0:
+        def keep_q(k):
+            qT[k] = per_batch.tile([P, TILES, P], BF16, name="qT", tag="qT", bufs=3 * H)
+            nc.scalar.copy(out=qT[k][:].bitcast(F32), in_=qT_ps[k][:].bitcast(F32))
+
+        def flip_q(k):
+            for step in range(TILES):
+                flip_q_tile(k, step)
+            keep_q(k)
+
+        def denominators(k):
+            b = k // H
+            if k % H == 0:
                 den_ps[b] = psum.tile([P, TILES, H], F32, name="den_ps", tag="den_ps")
-            for i in range(TILES):
+                den_sb[b] = per_batch.tile([P, TILES, H], F32, name="den_sb", tag="den_sb")
+                rden[b] = per_batch.tile([P, TILES, H], F32, name="rden", tag="rden")
+            for b, h, i in job_tiles(k):
                 nc.tensor.matmul(
                     den_ps[b][:, i, h : h + 1],
-                    lhsT=qT[b][:, h, i, :],
-                    rhs=ksT[:, unit : unit + 1],
+                    lhsT=qT_of(b, h, i),
+                    rhs=ksT[:, b * H + h : b * H + h + 1],
                     start=True,
                     stop=True,
                 )
-            if h == H - 1:
-                den_sb = per_batch.tile([P, TILES, H], F32, tag="den_sb")
-                nc.vector.tensor_scalar_add(out=den_sb[:], in0=den_ps[b][:], scalar1=EPS)
-                rden[b] = per_batch.tile([P, TILES, H], F32, name="rden", tag="rden")
-                nc.vector.reciprocal(out=rden[b][:], in_=den_sb[:])
+            ready = {0: slice(0, PAIR), 1: slice(PAIR, 2 * PAIR), H - 1: slice(2 * PAIR, TILES)}
+            if k < H and k in ready or k > H and k % H == H - 1:
+                tiles = ready[k] if k < H else slice(0, TILES)
+                nc.vector.tensor_scalar_add(out=den_sb[b][:, tiles, :], in0=den_ps[b][:, tiles, :], scalar1=EPS)
+                nc.vector.reciprocal(out=rden[b][:, tiles, :], in_=den_sb[b][:, tiles, :])
 
-        def read_out(n, unit):
+        def read_out(n, job):
             first, width = GROUPS[n]
             b, first = divmod(first, TILES)
             a_sb[n] = per_pair.tile([P, PAIR, E], BF16, name="a_sb", tag="a_sb")
@@ -154,10 +165,10 @@ def tile_lineartransformerblock_pc_t_kernel(tc, q_feat, vk, k_sum, Wo, bo, out):
                 hs_ps = psum.tile([P, H, D], F32, tag="hs_ps", bufs=3)
                 for h in range(H):
                     nc.tensor.matmul(
-                        hs_ps[:, h, :], lhsT=qT[b][:, h, i, :], rhs=vkT[b][:, h, :], start=True, stop=True
+                        hs_ps[:, h, :], lhsT=qT_of(b, h, i), rhs=vkT[b][:, h, :], start=True, stop=True
                     )
-                    if unit < HEADS:
-                        flip_q_tile(unit, j * H + h)
+                    if job < HEADS:
+                        flip_q_tile(job, j * H + h)
                 nc.vector.tensor_tensor(
                     out=a_sb[n][:, j, :].rearrange("p (u h k) -> p h u k", u=HALVES, h=H),
                     in0=hs_ps[:].rearrange("p h (u k) -> p h u k", u=HALVES),
@@ -222,63 +233,62 @@ def tile_lineartransformerblock_pc_t_kernel(tc, q_feat, vk, k_sum, Wo, bo, out):
             rows = out[b].rearrange("(p i) c -> p i c", i=TILES)
             nc.sync.dma_start(out=rows[:, first : first + width, :], in_=result)
 
+        wo_codes = const.tile([P, C], U32, align_bytes=64)
+        wo_scales = const.tile([P, C], U8, align_bytes=64)
+        bias = const.tile([P, C], F32)
+
+        def prepare_wo_and_bias():
+            wo_bank = psum.tile([P, HALVES, C], F32, tag="aT_ps")
+            for k in range(C_TILES):
+                words = wo_sb[:, k, :].bitcast(F32)
+                for u in range(HALVES):
+                    nc.tensor.transpose(
+                        wo_bank[:, u, k * P : (k + 1) * P], words[:, u : HALVES * P : HALVES], ident_words[:]
+                    )
+            wo_grouped = const.tile([P, C, PACK], BF16, align_bytes=64)
+            nc.vector.tensor_copy(out=wo_grouped[:].bitcast(F32), in_=wo_bank[:].rearrange("p u c -> p c u"))
+            bias_bank = psum.tile([P, PAIR, C], F32, tag="o_ps")
+            nc.tensor.matmul(bias_bank[:, 0, :], lhsT=ones[:], rhs=bo_row[:], start=True, stop=True)
+            nc.vector.tensor_copy(out=bias[:], in_=bias_bank[:, 0, :])
+            nc.vector.quantize_mx(
+                out=wo_codes[:].bitcast(FP8X4), scales=wo_scales[:], in_=wo_grouped[:].rearrange("p c t -> p (c t)")
+            )
+
         keep_clock(5)
         flip_vk(0)
-        flip_q(0)
         bank = psum.tile([P, TILES, P], BF16, tag="qT_ps", bufs=2)
         nc.tensor.transpose(bank[:, 0, :], ks_rows[:], ident[:])
         ksT = const.tile([P, HEADS], BF16)
         nc.scalar.copy(out=ksT[:], in_=bank[:, 0, 0:HEADS])
         keep_clock(1)
-        flip_q(1)
+        flip_q(0)
         keep_clock(1)
-
-        wo_bank = psum.tile([P, HALVES, C], F32, tag="aT_ps")
-        for k in range(C_TILES):
-            words = wo_sb[:, k, :].bitcast(F32)
-            for u in range(HALVES):
-                nc.tensor.transpose(
-                    wo_bank[:, u, k * P : (k + 1) * P], words[:, u : HALVES * P : HALVES], ident_words[:]
-                )
-        wo_grouped = const.tile([P, C, PACK], BF16, align_bytes=64)
-        nc.vector.tensor_copy(out=wo_grouped[:].bitcast(F32), in_=wo_bank[:].rearrange("p u c -> p c u"))
-        wo_codes = const.tile([P, C], U32, align_bytes=64)
-        wo_scales = const.tile([P, C], U8, align_bytes=64)
-        bias_bank = psum.tile([P, PAIR, C], F32, tag="o_ps")
-        nc.tensor.matmul(bias_bank[:, 0, :], lhsT=ones[:], rhs=bo_row[:], start=True, stop=True)
-        bias = const.tile([P, C], F32)
-        nc.vector.tensor_copy(out=bias[:], in_=bias_bank[:, 0, :])
-        nc.vector.quantize_mx(
-            out=wo_codes[:].bitcast(FP8X4), scales=wo_scales[:], in_=wo_grouped[:].rearrange("p c t -> p (c t)")
-        )
-
         denominators(0)
-        flip_q(2)
-        denominators(1)
-        keep_clock(1)
-        flip_q(3)
-        denominators(2)
-        denominators(3)
+        flip_q(1)
 
         for n in range(LAST):
             b, r = divmod(n, PAIRS)
-            if n >= 2:
-                quantise(n - 2)
             if n >= 3:
                 finish(n - 3)
-            read_out(n, n + H + 1)
+            if n >= 2:
+                quantise(n - 2)
+            jobs = [2 * n + 2, 2 * n + 3] if n < 3 else [n + H + 1]
+            read_out(n, jobs[0])
             if n == LAST - 1:
                 read_out(LAST, HEADS)
+            if jobs[0] < HEADS:
+                keep_q(jobs[0])
+            if n < 3:
+                flip_q(jobs[1])
             if n >= 1:
                 flip_a(n - 1)
-            if n == 0:
-                flip_q(H)
-            if n + H + 1 < HEADS:
-                keep_q(n + H + 1)
-            if r == 0 and b + 1 < B:
+            if r == 2 and b + 1 < B:
                 flip_vk(b + 1)
-            if n + H < HEADS:
-                denominators(n + H)
+            for k in [1] if n == 0 else [2 * n, 2 * n + 1] if n < 4 else [n + H]:
+                if k < HEADS:
+                    denominators(k)
+            if n == 0:
+                prepare_wo_and_bias()
             if n >= 2:
                 project(n - 2)
 

@@ -65,23 +65,32 @@ def tile_lineartransformerblock_pc_t_kernel(tc, q_feat, vk, k_sum, Wo, bo, out):
         nc.vector.memset(ones[:], 1.0)
 
         vk_sb = {}
-        q_sb = {}
+        q_tile = {}
 
         def load_vk(b):
             vk_sb[b] = loads.tile([P, H, D], BF16, name="vk_sb%d" % b)
             nc.sync.dma_start(out=vk_sb[b][:], in_=vk[b].rearrange("h n d -> n h d"))
 
+        def load_pairs(first, count):
+            tile = loads.tile([P, H, count * PAIR, D], BF16, name="q_pairs%d" % first)
+            rows = q_feat[0].rearrange("h (p i) d -> p h i d", i=TILES)
+            nc.sync.dma_start(out=tile[:], in_=rows[:, :, first * PAIR : (first + count) * PAIR, :])
+            for h in range(H):
+                for i in range(count * PAIR):
+                    q_tile[0, h, first * PAIR + i] = tile[:, h, i, :]
+
         def load_q(unit):
             b, h = divmod(unit, H)
-            q_sb[unit] = loads.tile([P, TILES, D], BF16, name="q_sb%d" % unit)
-            nc.sync.dma_start(out=q_sb[unit][:], in_=q_feat[b, h].rearrange("(p i) d -> p i d", i=TILES))
+            tile = loads.tile([P, TILES, D], BF16, name="q_sb%d" % unit)
+            nc.sync.dma_start(out=tile[:], in_=q_feat[b, h].rearrange("(p i) d -> p i d", i=TILES))
+            for i in range(TILES):
+                q_tile[b, h, i] = tile[:, i, :]
 
         load_vk(0)
-        load_q(0)
+        load_pairs(0, 1)
         nc.sync.dma_start(out=ks_rows[0:HEADS, :], in_=k_sum.rearrange("b h d -> (b h) d"))
-        load_q(1)
-        load_q(2)
-        load_q(3)
+        load_pairs(1, 1)
+        load_pairs(2, 2)
         wo_sb = const.tile([P, C_TILES, E], BF16)
         nc.sync.dma_start(out=wo_sb[:], in_=Wo.rearrange("(k p) e -> p k e", p=P))
         nc.sync.dma_start(out=bo_row[0:1, :], in_=bo.unsqueeze(0))
@@ -125,7 +134,7 @@ def tile_lineartransformerblock_pc_t_kernel(tc, q_feat, vk, k_sum, Wo, bo, out):
             if step == 0:
                 qT_ps[k] = psum.tile([P, TILES, P], BF16, name="qT_ps", tag="qT_ps", bufs=2)
             b, h, i = job_tiles(k)[step]
-            nc.tensor.transpose(qT_ps[k][:, step, :], q_sb[b * H + h][:, i, :], ident[:])
+            nc.tensor.transpose(qT_ps[k][:, step, :], q_tile[b, h, i], ident[:])
 
         def keep_q(k):
             qT[k] = per_batch.tile([P, TILES, P], BF16, name="qT", tag="qT", bufs=3 * H)
@@ -150,9 +159,8 @@ def tile_lineartransformerblock_pc_t_kernel(tc, q_feat, vk, k_sum, Wo, bo, out):
                     start=True,
                     stop=True,
                 )
-            ready = {0: slice(0, PAIR), 1: slice(PAIR, 2 * PAIR), H - 1: slice(2 * PAIR, TILES)}
-            if k < H and k in ready or k > H and k % H == H - 1:
-                tiles = ready[k] if k < H else slice(0, TILES)
+            if k < H or k % H == H - 1:
+                tiles = slice(k * PAIR, (k + 1) * PAIR) if k < H else slice(0, TILES)
                 nc.vector.tensor_scalar_add(out=den_sb[b][:, tiles, :], in0=den_ps[b][:, tiles, :], scalar1=EPS)
                 nc.vector.reciprocal(out=rden[b][:, tiles, :], in_=den_sb[b][:, tiles, :])
 
@@ -202,7 +210,7 @@ def tile_lineartransformerblock_pc_t_kernel(tc, q_feat, vk, k_sum, Wo, bo, out):
             )
 
         def project(n):
-            if GROUPS[n][1] < PAIR:
+            if n >= LAST - 2:
                 o_ps[n] = psum.tile([P, PAIR, C], F32, name="o_ps", tag="hs_ps", bufs=3)
             else:
                 o_ps[n] = psum.tile([P, PAIR, C], F32, name="o_ps", tag="o_ps")
@@ -225,7 +233,7 @@ def tile_lineartransformerblock_pc_t_kernel(tc, q_feat, vk, k_sum, Wo, bo, out):
             bias_rows = bias[:].unsqueeze(1).to_broadcast([P, width, C])
             product = o_ps[n][:, 0:width, :]
             result = o_sb[:, 0:width, :]
-            if n % 8 == 7 or n >= LAST - 2:
+            if n % 8 == 7 or n >= LAST - 3:
                 nc.vector.tensor_tensor(out=result, in0=product, in1=bias_rows, op=ADD)
             else:
                 nc.scalar.copy(out=result, in_=product)
@@ -254,17 +262,16 @@ def tile_lineartransformerblock_pc_t_kernel(tc, q_feat, vk, k_sum, Wo, bo, out):
                 out=wo_codes[:].bitcast(FP8X4), scales=wo_scales[:], in_=wo_grouped[:].rearrange("p c t -> p (c t)")
             )
 
-        keep_clock(5)
+        keep_clock(3)
         flip_vk(0)
+        flip_q(0)
+        keep_clock(1)
         bank = psum.tile([P, TILES, P], BF16, tag="qT_ps", bufs=2)
         nc.tensor.transpose(bank[:, 0, :], ks_rows[:], ident[:])
         ksT = const.tile([P, HEADS], BF16)
         nc.scalar.copy(out=ksT[:], in_=bank[:, 0, 0:HEADS])
         keep_clock(1)
-        flip_q(0)
-        keep_clock(1)
         denominators(0)
-        flip_q(1)
 
         for n in range(LAST):
             b, r = divmod(n, PAIRS)
@@ -272,30 +279,30 @@ def tile_lineartransformerblock_pc_t_kernel(tc, q_feat, vk, k_sum, Wo, bo, out):
                 finish(n - 3)
             if n >= 2:
                 quantise(n - 2)
-            jobs = [2 * n + 2, 2 * n + 3] if n < 3 else [n + H + 1]
+            jobs = [2 * n + 1, 2 * n + 2] if n < PAIRS else [n + H + 1]
             read_out(n, jobs[0])
             if n == LAST - 1:
                 read_out(LAST, HEADS)
             if jobs[0] < HEADS:
                 keep_q(jobs[0])
-            if n < 3:
-                flip_q(jobs[1])
+            for k in jobs[1:]:
+                flip_q(k)
             if n >= 1:
                 flip_a(n - 1)
             if r == 2 and b + 1 < B:
                 flip_vk(b + 1)
-            for k in [1] if n == 0 else [2 * n, 2 * n + 1] if n < 4 else [n + H]:
-                if k < HEADS:
-                    denominators(k)
             if n == 0:
                 prepare_wo_and_bias()
+            for k in [n + 1] if n < 3 else range(H, 2 * H) if n == 3 else [n + H]:
+                if k < HEADS:
+                    denominators(k)
             if n >= 2:
                 project(n - 2)
 
-        finish(LAST - 3)
         quantise(LAST - 2)
         for n in (LAST - 1, LAST):
             flip_a(n)
+        finish(LAST - 3)
         project(LAST - 2)
         for n in (LAST - 1, LAST):
             quantise(n)

@@ -233,7 +233,7 @@ def tile_lineartransformerblock_pc_t_kernel(tc, q_feat, vk, k_sum, Wo, bo, out):
             bias_rows = bias[:].unsqueeze(1).to_broadcast([P, width, C])
             product = o_ps[n][:, 0:width, :]
             result = o_sb[:, 0:width, :]
-            if n % 8 == 7 or n >= LAST - 3:
+            if n % 4 == 3 or n >= LAST - 3:
                 nc.vector.tensor_tensor(out=result, in0=product, in1=bias_rows, op=ADD)
             else:
                 nc.scalar.copy(out=result, in_=product)

from contextlib import ExitStack

import concourse.masks as masks
import concourse.mybir as mybir

BF16 = mybir.dt.bfloat16
F32 = mybir.dt.float32
U32 = mybir.dt.uint32
U8 = mybir.dt.uint8
FP8X4 = mybir.dt.float8_e4m3fn_x4
MULT = mybir.AluOpType.mult
ADD = mybir.AluOpType.add

B, H, S, D, C = 8, 4, 1024, 128, 256
E = H * D
EPS = 1e-15

P = 128
PACK = 4
HALVES = 2
TILES = S // P
PAIR = 2
PAIRS = TILES // PAIR
GROUPS = [(k * PAIR, PAIR) for k in range(B * PAIRS - 1)] + [(B * TILES - 2, 1), (B * TILES - 1, 1)]
LAST = len(GROUPS) - 1
HEADS = B * H
C_TILES = C // P

assert E == P * PACK
assert TILES == PAIR * H
assert H == PAIRS

FLOPS = 2 * B * S * E * C + 2 * B * H * S * D * D + 2 * B * H * S * D


def tile_lineartransformerblock_pc_t_kernel(tc, q_feat, vk, k_sum, Wo, bo, out):
    nc = tc.nc
    with ExitStack() as ctx:
        const = ctx.enter_context(tc.tile_pool(name="const", bufs=1))
        loads = ctx.enter_context(tc.tile_pool(name="loads", bufs=1))
        per_batch = ctx.enter_context(tc.tile_pool(name="per_batch", bufs=3))
        per_pair = ctx.enter_context(tc.tile_pool(name="per_pair", bufs=3))
        psum = ctx.enter_context(tc.psum_pool(name="psum", bufs=1))
        ctx.enter_context(tc.manual_schedule())

        ident = const.tile([P, P], BF16)
        masks.make_identity(nc, ident[:])
        ident_words = const.tile([P, P], F32)
        masks.make_identity(nc, ident_words[:])

        idle_rows = const.tile([P, PAIR * C], BF16)
        nc.vector.memset(idle_rows[:], 0.0)

        def keep_clock(times):
            for k in range(times):
                bank = psum.tile([P, PAIR * C], F32, tag="hs_ps", bufs=3)
                nc.tensor.matmul(bank[:], lhsT=idle_rows[:, 0:P], rhs=idle_rows[:], start=True, stop=True)

        ks_rows = const.tile([P, D], BF16)
        nc.vector.memset(ks_rows[:], 0.0)

        bo_row = const.tile([P, C], BF16)
        nc.vector.memset(bo_row[:], 0.0)
        ones = const.tile([P, P], BF16)
        nc.vector.memset(ones[:], 1.0)

        vk_sb = {}
        q_tile = {}

        def load_vk(b):
            vk_sb[b] = loads.tile([P, H, D], BF16, name="vk_sb%d" % b)
            nc.sync.dma_start(out=vk_sb[b][:], in_=vk[b].rearrange("h n d -> n h d"))

        def load_pairs(first, count):
            tile = loads.tile([P, H, count * PAIR, D], BF16, name="q_pairs%d" % first)
            rows = q_feat[0].rearrange("h (p i) d -> p h i d", i=TILES)
            nc.sync.dma_start(out=tile[:], in_=rows[:, :, first * PAIR : (first + count) * PAIR, :])
            for h in range(H):
                for i in range(count * PAIR):
                    q_tile[0, h, first * PAIR + i] = tile[:, h, i, :]

        def load_q(unit):
            b, h = divmod(unit, H)
            tile = loads.tile([P, TILES, D], BF16, name="q_sb%d" % unit)
            nc.sync.dma_start(out=tile[:], in_=q_feat[b, h].rearrange("(p i) d -> p i d", i=TILES))
            for i in range(TILES):
                q_tile[b, h, i] = tile[:, i, :]

        load_vk(0)
        load_pairs(0, 1)
        nc.sync.dma_start(out=ks_rows[0:HEADS, :], in_=k_sum.rearrange("b h d -> (b h) d"))
        load_pairs(1, 1)
        load_pairs(2, 2)
        wo_sb = const.tile([P, C_TILES, E], BF16)
        nc.sync.dma_start(out=wo_sb[:], in_=Wo.rearrange("(k p) e -> p k e", p=P))
        nc.sync.dma_start(out=bo_row[0:1, :], in_=bo.unsqueeze(0))
        for b in range(1, B):
            load_vk(b)
            for h in range(H):
                load_q(b * H + h)

        vkT = {}
        qT_ps = {}
        qT = {}
        den_ps = {}
        den_sb = {}
        rden = {}
        a_sb = {}
        grouped = {}
        codes = {}
        scales = {}
        o_ps = {}

        def flip_vk(b):
            bank = psum.tile([P, TILES, P], BF16, tag="qT_ps", bufs=2)
            for h in range(H):
                nc.tensor.transpose(bank[:, h, :], vk_sb[b][:, h, :], ident[:])
            vkT[b] = per_batch.tile([P, H, D], BF16, name="vkT", tag="vkT")
            nc.scalar.copy(
                out=vkT[b][:].bitcast(F32).rearrange("p h (u m) -> p h u m", u=HALVES),
                in_=bank[:, 0:H, :].bitcast(F32).rearrange("p h (m u) -> p h u m", u=HALVES),
            )

        def job_tiles(k):
            if k < H:
                return [(0, h, k * PAIR + j) for h in range(H) for j in range(PAIR)]
            return [(k // H, k % H, i) for i in range(TILES)]

        def qT_of(b, h, i):
            k = i // PAIR if b == 0 else b * H + h
            return qT[k][:, job_tiles(k).index((b, h, i)), :]

        def flip_q_tile(k, step):
            if step == 0:
                qT_ps[k] = psum.tile([P, TILES, P], BF16, name="qT_ps", tag="qT_ps", bufs=2)
            b, h, i = job_tiles(k)[step]
            nc.tensor.transpose(qT_ps[k][:, step, :], q_tile[b, h, i], ident[:])

        def keep_q(k):
            qT[k] = per_batch.tile([P, TILES, P], BF16, name="qT", tag="qT", bufs=3 * H)
            nc.scalar.copy(out=qT[k][:].bitcast(F32), in_=qT_ps[k][:].bitcast(F32))

        def flip_q(k):
            for step in range(TILES):
                flip_q_tile(k, step)
            keep_q(k)

        def denominators(k):
            b = k // H
            if k % H == 0:
                den_ps[b] = psum.tile([P, TILES, H], F32, name="den_ps", tag="den_ps")
                den_sb[b] = per_batch.tile([P, TILES, H], F32, name="den_sb", tag="den_sb")
                rden[b] = per_batch.tile([P, TILES, H], F32, name="rden", tag="rden")
            for b, h, i in job_tiles(k):
                nc.tensor.matmul(
                    den_ps[b][:, i, h : h + 1],
                    lhsT=qT_of(b, h, i),
                    rhs=ksT[:, b * H + h : b * H + h + 1],
                    start=True,
                    stop=True,
                )
            if k < H or k % H == H - 1:
                tiles = slice(k * PAIR, (k + 1) * PAIR) if k < H else slice(0, TILES)
                nc.vector.tensor_scalar_add(out=den_sb[b][:, tiles, :], in0=den_ps[b][:, tiles, :], scalar1=EPS)
                nc.vector.reciprocal(out=rden[b][:, tiles, :], in_=den_sb[b][:, tiles, :])

        def read_out(n, job):
            first, width = GROUPS[n]
            b, first = divmod(first, TILES)
            a_sb[n] = per_pair.tile([P, PAIR, E], BF16, name="a_sb", tag="a_sb")
            for j in range(width):
                i = first + j
                hs_ps = psum.tile([P, H, D], F32, tag="hs_ps", bufs=3)
                for h in range(H):
                    nc.tensor.matmul(
                        hs_ps[:, h, :], lhsT=qT_of(b, h, i), rhs=vkT[b][:, h, :], start=True, stop=True
                    )
                    if job < HEADS:
                        flip_q_tile(job, j * H + h)
                nc.vector.tensor_tensor(
                    out=a_sb[n][:, j, :].rearrange("p (u h k) -> p h u k", u=HALVES, h=H),
                    in0=hs_ps[:].rearrange("p h (u k) -> p h u k", u=HALVES),
                    in1=rden[b][:, i, :].unsqueeze(2).unsqueeze(3).to_broadcast([P, H, HALVES, D // HALVES]),
                    op=MULT,
                )

        def flip_a(n):
            width = GROUPS[n][1]
            if GROUPS[n][1] < PAIR:
                bank = psum.tile([P, PAIR, HALVES, P], F32, tag="qT_ps", bufs=2)
            else:
                bank = psum.tile([P, PAIR, HALVES, P], F32, tag="aT_ps")
            for j in range(width):
                words = a_sb[n][:, j, :].bitcast(F32)
                for u in range(HALVES):
                    nc.tensor.transpose(bank[:, j, u, :], words[:, u * P : (u + 1) * P], ident_words[:])
            grouped[n] = per_pair.tile([P, PAIR, P, PACK], BF16, name="grouped", tag="grouped", align_bytes=64)
            nc.scalar.copy(
                out=grouped[n][:, 0:width, :, :].bitcast(F32), in_=bank[:, 0:width, :, :].rearrange("p j u s -> p j s u")
            )

        def quantise(n):
            tokens = slice(0, GROUPS[n][1] * P)
            codes[n] = per_pair.tile([P, PAIR * P], U32, name="codes", tag="codes", align_bytes=64)
            scales[n] = per_pair.tile([P, PAIR * P], U8, name="scales", tag="scales", align_bytes=64)
            nc.vector.quantize_mx(
                out=codes[n][:, tokens].bitcast(FP8X4),
                scales=scales[n][:, tokens],
                in_=grouped[n][:, 0 : GROUPS[n][1], :, :].rearrange("p j s t -> p (j s t)"),
            )

        def project(n):
            if n >= LAST - 2:
                o_ps[n] = psum.tile([P, PAIR, C], F32, name="o_ps", tag="hs_ps", bufs=3)
            else:
                o_ps[n] = psum.tile([P, PAIR, C], F32, name="o_ps", tag="o_ps")
            for j in range(GROUPS[n][1]):
                tokens = slice(j * P, (j + 1) * P)
                nc.tensor.matmul_mx(
                    out=o_ps[n][:, j, :],
                    lhsT=codes[n][:, tokens].bitcast(FP8X4),
                    lhsT_scale=scales[n][:, tokens],
                    rhs=wo_codes[:].bitcast(FP8X4),
                    rhs_scale=wo_scales[:],
                    start=True,
                    stop=True,
                )

        def finish(n):
            first, width = GROUPS[n]
            b, first = divmod(first, TILES)
            o_sb = per_pair.tile([P, PAIR, C], F32, tag="o_sb", bufs=12)
            bias_rows = bias[:].unsqueeze(1).to_broadcast([P, width, C])
            product = o_ps[n][:, 0:width, :]
            result = o_sb[:, 0:width, :]
            if n % 4 == 3 or n >= LAST - 3:
                nc.vector.tensor_tensor(out=result, in0=product, in1=bias_rows, op=ADD)
            else:
                nc.scalar.copy(out=result, in_=product)
                nc.gpsimd.tensor_tensor(out=result, in0=result, in1=bias_rows, op=ADD)
            rows = out[b].rearrange("(p i) c -> p i c", i=TILES)
            nc.sync.dma_start(out=rows[:, first : first + width, :], in_=result)

        wo_codes = const.tile([P, C], U32, align_bytes=64)
        wo_scales = const.tile([P, C], U8, align_bytes=64)
        bias = const.tile([P, C], F32)

        def prepare_wo_and_bias():
            wo_bank = psum.tile([P, HALVES, C], F32, tag="aT_ps")
            for k in range(C_TILES):
                words = wo_sb[:, k, :].bitcast(F32)
                for u in range(HALVES):
                    nc.tensor.transpose(
                        wo_bank[:, u, k * P : (k + 1) * P], words[:, u : HALVES * P : HALVES], ident_words[:]
                    )
            wo_grouped = const.tile([P, C, PACK], BF16, align_bytes=64)
            nc.vector.tensor_copy(out=wo_grouped[:].bitcast(F32), in_=wo_bank[:].rearrange("p u c -> p c u"))
            bias_bank = psum.tile([P, PAIR, C], F32, tag="o_ps")
            nc.tensor.matmul(bias_bank[:, 0, :], lhsT=ones[:], rhs=bo_row[:], start=True, stop=True)
            nc.vector.tensor_copy(out=bias[:], in_=bias_bank[:, 0, :])
            nc.vector.quantize_mx(
                out=wo_codes[:].bitcast(FP8X4), scales=wo_scales[:], in_=wo_grouped[:].rearrange("p c t -> p (c t)")
            )

        keep_clock(3)
        flip_vk(0)
        flip_q(0)
        keep_clock(1)
        bank = psum.tile([P, TILES, P], BF16, tag="qT_ps", bufs=2)
        nc.tensor.transpose(bank[:, 0, :], ks_rows[:], ident[:])
        ksT = const.tile([P, HEADS], BF16)
        nc.scalar.copy(out=ksT[:], in_=bank[:, 0, 0:HEADS])
        keep_clock(1)
        denominators(0)

        for n in range(LAST):
            b, r = divmod(n, PAIRS)
            if n >= 3:
                finish(n - 3)
            if n >= 2:
                quantise(n - 2)
            jobs = [2 * n + 1, 2 * n + 2] if n < PAIRS else [n + H + 1]
            read_out(n, jobs[0])
            if n == LAST - 1:
                read_out(LAST, HEADS)
            if jobs[0] < HEADS:
                keep_q(jobs[0])
            for k in jobs[1:]:
                flip_q(k)
            if n >= 1:
                flip_a(n - 1)
            if r == 2 and b + 1 < B:
                flip_vk(b + 1)
            if n == 0:
                prepare_wo_and_bias()
            for k in [n + 1] if n < 3 else range(H, 2 * H) if n == 3 else [n + H]:
                if k < HEADS:
                    denominators(k)
            if n >= 2:
                project(n - 2)

        quantise(LAST - 2)
        for n in (LAST - 1, LAST):
            flip_a(n)
        finish(LAST - 3)
        project(LAST - 2)
        for n in (LAST - 1, LAST):
            quantise(n)
            project(n)
        for n in (LAST - 2, LAST - 1, LAST):
            finish(n)
